import numpy as np
import ml_dtypes


def mxq(x, axis, fmt="e4m3"):
    dtype, down = {"e4m3": (ml_dtypes.float8_e4m3fn, 7), "e5m2": (ml_dtypes.float8_e5m2, 14)}[fmt]
    v = np.moveaxis(np.asarray(x, np.float32).astype(ml_dtypes.bfloat16).astype(np.float64), axis, -1)
    blocks = v.reshape(v.shape[:-1] + (-1, 32))
    amax = np.abs(blocks).max(-1, keepdims=True)
    byte = np.maximum(np.where(amax > 0, np.frexp(amax)[1] - 1 + 127, 0) - down, 1)
    scale = np.exp2(byte - 127.0)
    codes = (blocks / scale).astype(np.float32).astype(dtype).astype(np.float64)
    return np.moveaxis((codes * scale).reshape(v.shape), -1, axis)


WIDE = False


def mx_kscale(k):
    if not WIDE:
        return np.ones(k)
    levels = np.array([20, -20, 10, -10, 0])
    a = np.random.permutation(np.resize(levels, k // 512 * 4)).reshape(k // 512, 4)
    idx = np.arange(k)
    return np.exp2(a[idx // 512, idx % 128 // 32])


BF16 = ml_dtypes.bfloat16


def bf(x):
    return np.asarray(x, np.float32).astype(BF16)


def f64(x):
    return np.asarray(x).astype(np.float64)


B, T, G, I, H = 4, 256, 8, 512, 512
N = B * T


def setup_inputs():
    s = mx_kscale(N).reshape(B, T, 1)
    x = np.random.standard_normal((B, T, G, I)).reshape(B, T, G * I) * s
    W = np.random.standard_normal((G, H, I)) / np.sqrt(I)
    b = np.random.standard_normal((G, H)) * 0.5
    g = np.random.standard_normal((B, T, G * H)) * np.exp2(np.random.randint(-12, 1, (B, T, 1))) / s
    return {"x": bf(x), "W": bf(W), "b": bf(b), "grad_out": bf(g)}


def reference(x, W, b, grad_out):
    xq = mxq(f64(x).reshape(N, G, I), 0, "e4m3")
    gq = mxq(f64(grad_out).reshape(N, H, G), 0, "e5m2")
    return gq.transpose(2, 1, 0) @ xq.transpose(1, 0, 2)

@@ -1,0 +1,158 @@
+from contextlib import ExitStack
+
+import concourse.mybir as mybir
+
+FLOPS = 2 * 8 * 512 * 512 * 1024
+BYTES = 3 * 8 * 1024 * 1024
+
+BF16 = mybir.dt.bfloat16
+F32 = mybir.dt.float32
+U32 = mybir.dt.uint32
+U8 = mybir.dt.uint8
+E4M3 = mybir.dt.float8_e4m3fn_x4
+E5M2 = mybir.dt.float8_e5m2_x4
+
+P = 128
+PACK = 4
+CW = 2048
+
+CHUNKS = [
+    ("g", 0, 0), ("g", 1, 0), ("x", 0, 0), ("x", 1, 0),
+    ("g", 0, 1), ("g", 1, 1), ("x", 0, 1), ("x", 1, 1),
+]
+SCALAR_COPIES = [(3,), (2, 3), (3,), (3,), (2, 3), (2, 3), (3,), (3,)]
+RAW_BUFS = 5
+VECTOR_EVACS = ()
+
+
+def tile_groupedlinear_kernel(tc, x, W, b, grad_out, out):
+    nc = tc.nc
+    xv = x.flatten_outer_dims().rearrange("(c p t) f -> c p t f", p=P, t=PACK)
+    gv = grad_out.flatten_outer_dims().rearrange("(c p t) f -> c p t f", p=P, t=PACK)
+    ov = out.rearrange("g (q m r) i -> g q m (r i)", q=2, r=2)
+
+    with ExitStack() as ctx:
+        raw_pool = ctx.enter_context(tc.tile_pool(name="raw", bufs=RAW_BUFS))
+        half_pool = ctx.enter_context(tc.tile_pool(name="rawh", bufs=2))
+        keep = ctx.enter_context(tc.tile_pool(name="keep", bufs=1))
+        grp_pool = ctx.enter_context(tc.tile_pool(name="grp", bufs=4))
+        stage_pool = ctx.enter_context(tc.tile_pool(name="stage", bufs=4))
+        psum = ctx.enter_context(tc.psum_pool(name="psum", bufs=8))
+
+        codes = {}
+        planes = {}
+        for kind, c, half in CHUNKS:
+            for j in range(2):
+                codes[(kind, c, half, j)] = keep.tile(
+                    [P, 1024], U32, name="codes_%s%d%d%d" % (kind, c, half, j), align_bytes=64)
+                planes[(kind, c, half, j)] = keep.tile(
+                    [P, 1024], U8, name="plane_%s%d%d%d" % (kind, c, half, j), align_bytes=64)
+
+        raws = {}
+
+        def load(k):
+            kind, c, half = CHUNKS[k]
+            src = gv if kind == "g" else xv
+            if k == 0:
+                parts = []
+                for s in range(2):
+                    rh = half_pool.tile([P, PACK, CW // 2], BF16, name="rawh")
+                    lo = half * CW + s * (CW // 2)
+                    nc.sync.dma_start(out=rh[:], in_=src[c][:, :, lo:lo + CW // 2])
+                    parts.append(rh)
+                raws[k] = parts
+            else:
+                rw = raw_pool.tile([P, PACK, CW], BF16, name="raw")
+                nc.sync.dma_start(out=rw[:], in_=src[c][:, :, half * CW:(half + 1) * CW])
+                raws[k] = [rw]
+
+        def copy(on_scalar, dst, src):
+            if on_scalar:
+                nc.scalar.copy(out=dst, in_=src)
+            else:
+                nc.vector.tensor_copy(out=dst, in_=src)
+
+        grouped = {}
+
+        def regroup(k):
+            kind, c, half = CHUNKS[k]
+            parts = raws[k]
+            tiles = []
+            for j in range(2):
+                gt = grp_pool.tile([P, 4096], BF16, name="grp", align_bytes=64)
+                tiles.append(gt)
+            grouped[k] = tiles
+            n = len(parts)
+            for s in range(n):
+                for idx in range(4):
+                    j, a = idx // 2, idx % 2
+                    on_scalar = idx in SCALAR_COPIES[k]
+                    if kind == "g":
+                        nm = P // n
+                        sv = parts[s][:].rearrange("p t (m r a i) -> p r a m t i", r=2, a=2, i=4)
+                        dv = tiles[j][:].rearrange("p (a i m t) -> p a m t i", a=2, i=4, t=PACK)
+                        copy(on_scalar, dv[:, a, s * nm:(s + 1) * nm], sv[:, j, a])
+                    else:
+                        sv = parts[s][:].rearrange("p t (g c i) -> p g c t i", g=4, i=4)
+                        dv = tiles[j][:].rearrange("p (g c i t) -> p g c t i", g=2, i=4, t=PACK)
+                        copy(on_scalar, dv[:, a], sv[:, idx])
+
+        def quantise(k, j):
+            kind, c, half = CHUNKS[k]
+            fmt = E5M2 if kind == "g" else E4M3
+            nc.vector.quantize_mx(
+                out=codes[(kind, c, half, j)][:].bitcast(fmt),
+                scales=planes[(kind, c, half, j)][:],
+                in_=grouped[k][j][:],
+            )
+
+        count = [0]
+
+        def product(g, q):
+            st = stage_pool.tile([P, 1024], F32, name="stage")
+            for r in range(2):
+                acc = psum.tile([P, 512], F32, name="acc")
+                for c in range(2):
+                    kx = ("x", c, g // 4, (g % 4) // 2)
+                    kg = ("g", c, q, r)
+                    xs = slice((g % 2) * 512, (g % 2) * 512 + 512)
+                    gs = slice(g * P, (g + 1) * P)
+                    nc.tensor.matmul_mx(
+                        out=acc[:],
+                        lhsT=codes[kg][:, gs].bitcast(E5M2),
+                        lhsT_scale=planes[kg][:, gs],
+                        rhs=codes[kx][:, xs].bitcast(E4M3),
+                        rhs_scale=planes[kx][:, xs],
+                        start=(c == 0),
+                        stop=(c == 1),
+                    )
+                copy(count[0] not in VECTOR_EVACS, st[:, r * 512:(r + 1) * 512], acc[:])
+                count[0] += 1
+            nc.sync.dma_start(out=ov[g, q], in_=st[:])
+
+        for k in range(RAW_BUFS + 1):
+            load(k)
+        for k in range(8):
+            regroup(k)
+            if k + RAW_BUFS + 1 < 8:
+                load(k + RAW_BUFS + 1)
+            if k > 0:
+                quantise(k - 1, 1)
+                if k - 1 == 3:
+                    product(2, 0)
+                    product(3, 0)
+                if k - 1 == 5:
+                    for g in range(4):
+                        product(g, 1)
+            quantise(k, 0)
+            if k == 3:
+                product(0, 0)
+                product(1, 0)
+            if k == 7:
+                for g in (4, 5):
+                    for q in range(2):
+                        product(g, q)
+        quantise(7, 1)
+        for g in (6, 7):
+            for q in range(2):
+                product(g, q)

@@ -16,13 +16,14 @@ P = 128
 PACK = 4
 CW = 2048
 
-CHUNKS = [
-    ("g", 0, 0), ("g", 1, 0), ("x", 0, 0), ("x", 1, 0),
-    ("g", 0, 1), ("g", 1, 1), ("x", 0, 1), ("x", 1, 1),
-]
-SCALAR_COPIES = [(3,), (2, 3), (3,), (3,), (2, 3), (2, 3), (3,), (3,)]
-RAW_BUFS = 5
-VECTOR_EVACS = ()
+CHUNKS = [("g", 0, 0, 4), ("g", 1, 0, 2), ("x", 0, 0, 1), ("x", 1, 0, 1), ("g", 0, 1, 1), ("g", 1, 1, 1), ("x", 0, 1, 1), ("x", 1, 1, 1)]
+SCALAR_COPIES = [(2, 3), (2, 3), (2, 3), (2, 3), (3,), (3,), (0, 1, 2, 3), ()]
+VECTOR_EVACS = (16, 17, 20, 21, 24, 25, 28, 29)
+RAW_BUFS = {1: 4, 2: 2, 4: 4}
+GRP_BUFS = 4
+STAGE_BUFS = 6
+LAG = 1
+PINNED = False
 
 
 def tile_groupedlinear_kernel(tc, x, W, b, grad_out, out):
@@ -32,16 +33,19 @@ def tile_groupedlinear_kernel(tc, x, W, b, grad_out, out):
     ov = out.rearrange("g (q m r) i -> g q m (r i)", q=2, r=2)
 
     with ExitStack() as ctx:
-        raw_pool = ctx.enter_context(tc.tile_pool(name="raw", bufs=RAW_BUFS))
-        half_pool = ctx.enter_context(tc.tile_pool(name="rawh", bufs=2))
+        raw_pools = {}
+        for n in (1, 2, 4):
+            raw_pools[n] = ctx.enter_context(tc.tile_pool(name="raw%d" % n, bufs=RAW_BUFS[n]))
         keep = ctx.enter_context(tc.tile_pool(name="keep", bufs=1))
-        grp_pool = ctx.enter_context(tc.tile_pool(name="grp", bufs=4))
-        stage_pool = ctx.enter_context(tc.tile_pool(name="stage", bufs=4))
+        grp_pool = ctx.enter_context(tc.tile_pool(name="grp", bufs=GRP_BUFS))
+        stage_pool = ctx.enter_context(tc.tile_pool(name="stage", bufs=STAGE_BUFS))
         psum = ctx.enter_context(tc.psum_pool(name="psum", bufs=8))
+        if PINNED:
+            ctx.enter_context(tc.manual_schedule())
 
         codes = {}
         planes = {}
-        for kind, c, half in CHUNKS:
+        for kind, c, half, n in CHUNKS:
             for j in range(2):
                 codes[(kind, c, half, j)] = keep.tile(
                     [P, 1024], U32, name="codes_%s%d%d%d" % (kind, c, half, j), align_bytes=64)
@@ -49,22 +53,17 @@ def tile_groupedlinear_kernel(tc, x, W, b, grad_out, out):
                     [P, 1024], U8, name="plane_%s%d%d%d" % (kind, c, half, j), align_bytes=64)
 
         raws = {}
-
-        def load(k):
-            kind, c, half = CHUNKS[k]
+        for k in range(len(CHUNKS)):
+            kind, c, half, n = CHUNKS[k]
             src = gv if kind == "g" else xv
-            if k == 0:
-                parts = []
-                for s in range(2):
-                    rh = half_pool.tile([P, PACK, CW // 2], BF16, name="rawh")
-                    lo = half * CW + s * (CW // 2)
-                    nc.sync.dma_start(out=rh[:], in_=src[c][:, :, lo:lo + CW // 2])
-                    parts.append(rh)
-                raws[k] = parts
-            else:
-                rw = raw_pool.tile([P, PACK, CW], BF16, name="raw")
-                nc.sync.dma_start(out=rw[:], in_=src[c][:, :, half * CW:(half + 1) * CW])
-                raws[k] = [rw]
+            w = CW // n
+            parts = []
+            for s in range(n):
+                rw = raw_pools[n].tile([P, PACK, w], BF16, name="raw%d" % n)
+                lo = half * CW + s * w
+                nc.sync.dma_start(out=rw[:], in_=src[c][:, :, lo:lo + w])
+                parts.append(rw)
+            raws[k] = parts
 
         def copy(on_scalar, dst, src):
             if on_scalar:
@@ -74,85 +73,81 @@ def tile_groupedlinear_kernel(tc, x, W, b, grad_out, out):
 
         grouped = {}
 
-        def regroup(k):
-            kind, c, half = CHUNKS[k]
-            parts = raws[k]
-            tiles = []
-            for j in range(2):
-                gt = grp_pool.tile([P, 4096], BF16, name="grp", align_bytes=64)
-                tiles.append(gt)
-            grouped[k] = tiles
-            n = len(parts)
+        def regroup(k, j):
+            kind, c, half, n = CHUNKS[k]
+            gt = grp_pool.tile([P, 4096], BF16, name="grp", align_bytes=64)
+            grouped[(k, j)] = gt
             for s in range(n):
-                for idx in range(4):
-                    j, a = idx // 2, idx % 2
-                    on_scalar = idx in SCALAR_COPIES[k]
+                for a in range(2):
+                    on_scalar = (2 * j + a) in SCALAR_COPIES[k]
                     if kind == "g":
                         nm = P // n
-                        sv = parts[s][:].rearrange("p t (m r a i) -> p r a m t i", r=2, a=2, i=4)
-                        dv = tiles[j][:].rearrange("p (a i m t) -> p a m t i", a=2, i=4, t=PACK)
+                        sv = raws[k][s][:].rearrange("p t (m r a i) -> p r a m t i", r=2, a=2, i=4)
+                        dv = gt[:].rearrange("p (a i m t) -> p a m t i", a=2, i=4, t=PACK)
                         copy(on_scalar, dv[:, a, s * nm:(s + 1) * nm], sv[:, j, a])
                     else:
-                        sv = parts[s][:].rearrange("p t (g c i) -> p g c t i", g=4, i=4)
-                        dv = tiles[j][:].rearrange("p (g c i t) -> p g c t i", g=2, i=4, t=PACK)
-                        copy(on_scalar, dv[:, a], sv[:, idx])
+                        sv = raws[k][s][:].rearrange("p t (g c i) -> p g c t i", g=4, i=4)
+                        dv = gt[:].rearrange("p (g c i t) -> p g c t i", g=2, i=4, t=PACK)
+                        copy(on_scalar, dv[:, a], sv[:, 2 * j + a])
 
-        def quantise(k, j):
-            kind, c, half = CHUNKS[k]
-            fmt = E5M2 if kind == "g" else E4M3
-            nc.vector.quantize_mx(
-                out=codes[(kind, c, half, j)][:].bitcast(fmt),
-                scales=planes[(kind, c, half, j)][:],
-                in_=grouped[k][j][:],
-            )
-
+        ready = set()
+        stored = set()
         count = [0]
 
-        def product(g, q):
-            st = stage_pool.tile([P, 1024], F32, name="stage")
-            for r in range(2):
-                acc = psum.tile([P, 512], F32, name="acc")
-                for c in range(2):
-                    kx = ("x", c, g // 4, (g % 4) // 2)
-                    kg = ("g", c, q, r)
-                    xs = slice((g % 2) * 512, (g % 2) * 512 + 512)
-                    gs = slice(g * P, (g + 1) * P)
-                    nc.tensor.matmul_mx(
-                        out=acc[:],
-                        lhsT=codes[kg][:, gs].bitcast(E5M2),
-                        lhsT_scale=planes[kg][:, gs],
-                        rhs=codes[kx][:, xs].bitcast(E4M3),
-                        rhs_scale=planes[kx][:, xs],
-                        start=(c == 0),
-                        stop=(c == 1),
-                    )
-                copy(count[0] not in VECTOR_EVACS, st[:, r * 512:(r + 1) * 512], acc[:])
-                count[0] += 1
-            nc.sync.dma_start(out=ov[g, q], in_=st[:])
+        def products():
+            for g in range(8):
+                for q in range(2):
+                    if (g, q) in stored:
+                        continue
+                    need = [("x", c, g // 4, (g % 4) // 2, g % 2) for c in range(2)]
+                    need += [("g", c, q, r, a) for c in range(2) for r in range(2) for a in range(2)]
+                    if not all(u in ready for u in need):
+                        continue
+                    stored.add((g, q))
+                    st = stage_pool.tile([P, 1024], F32, name="stage")
+                    for r in range(2):
+                        acc = psum.tile([P, 512], F32, name="acc")
+                        for c in range(2):
+                            kx = ("x", c, g // 4, (g % 4) // 2)
+                            kg = ("g", c, q, r)
+                            xs = slice((g % 2) * 512, (g % 2) * 512 + 512)
+                            gs = slice(g * P, (g + 1) * P)
+                            nc.tensor.matmul_mx(
+                                out=acc[:],
+                                lhsT=codes[kg][:, gs].bitcast(E5M2),
+                                lhsT_scale=planes[kg][:, gs],
+                                rhs=codes[kx][:, xs].bitcast(E4M3),
+                                rhs_scale=planes[kx][:, xs],
+                                start=(c == 0),
+                                stop=(c == 1),
+                            )
+                        copy(count[0] not in VECTOR_EVACS, st[:, r * 512:(r + 1) * 512], acc[:])
+                        count[0] += 1
+                    nc.sync.dma_start(out=ov[g, q], in_=st[:])
 
-        for k in range(RAW_BUFS + 1):
-            load(k)
-        for k in range(8):
-            regroup(k)
-            if k + RAW_BUFS + 1 < 8:
-                load(k + RAW_BUFS + 1)
-            if k > 0:
-                quantise(k - 1, 1)
-                if k - 1 == 3:
-                    product(2, 0)
-                    product(3, 0)
-                if k - 1 == 5:
-                    for g in range(4):
-                        product(g, 1)
-            quantise(k, 0)
-            if k == 3:
-                product(0, 0)
-                product(1, 0)
-            if k == 7:
-                for g in (4, 5):
-                    for q in range(2):
-                        product(g, q)
-        quantise(7, 1)
-        for g in (6, 7):
-            for q in range(2):
-                product(g, q)
+        def quantise(k, j):
+            kind, c, half, n = CHUNKS[k]
+            fmt = E5M2 if kind == "g" else E4M3
+            key = (kind, c, half, j)
+            last = k == len(CHUNKS) - 1 and j == 1
+            pieces = 2 if last else 1
+            w = 1024 // pieces
+            for h in range(pieces):
+                nc.vector.quantize_mx(
+                    out=codes[key][:, h * w:(h + 1) * w].bitcast(fmt),
+                    scales=planes[key][:, h * w:(h + 1) * w],
+                    in_=grouped[(k, j)][:, 4 * h * w:4 * (h + 1) * w],
+                )
+                if pieces == 2:
+                    ready.add(key + (h,))
+                else:
+                    ready.add(key + (0,))
+                    ready.add(key + (1,))
+                products()
+
+        units = [(k, j) for k in range(len(CHUNKS)) for j in range(2)]
+        for u in range(len(units) + LAG):
+            if u < len(units):
+                regroup(units[u][0], units[u][1])
+            if u >= LAG:
+                quantise(units[u - LAG][0], units[u - LAG][1])

@@ -14,16 +14,25 @@ E5M2 = mybir.dt.float8_e5m2_x4
 
 P = 128
 PACK = 4
-CW = 2048
 
-CHUNKS = [("g", 0, 0, 4), ("g", 1, 0, 2), ("x", 0, 0, 1), ("x", 1, 0, 1), ("g", 0, 1, 1), ("g", 1, 1, 1), ("x", 0, 1, 1), ("x", 1, 1, 1)]
-SCALAR_COPIES = [(2, 3), (2, 3), (2, 3), (2, 3), (3,), (3,), (0, 1, 2, 3), ()]
-VECTOR_EVACS = (16, 17, 20, 21, 24, 25, 28, 29)
-RAW_BUFS = {1: 4, 2: 2, 4: 4}
-GRP_BUFS = 4
+LOADS = [
+    ("g", 0, 0, 512), ("g", 0, 512, 512), ("g", 0, 1024, 512), ("g", 0, 1536, 512),
+    ("g", 1, 0, 1024), ("g", 1, 1024, 1024), ("x", 0, 0, 2048), ("x", 1, 0, 2048),
+    ("g", 0, 2048, 2048), ("g", 1, 2048, 2048),
+    ("x", 0, 2048, 1024), ("x", 1, 2048, 1024), ("x", 0, 3072, 1024), ("x", 1, 3072, 1024),
+]
+UNITS = [
+    ("g", 0, 0, 0), ("g", 0, 0, 1), ("g", 1, 0, 0), ("g", 1, 0, 1),
+    ("x", 0, 0), ("x", 0, 1), ("x", 1, 0), ("x", 1, 1),
+    ("g", 0, 1, 0), ("g", 0, 1, 1), ("g", 1, 1, 0), ("g", 1, 1, 1),
+    ("x", 0, 2), ("x", 1, 2), ("x", 0, 3), ("x", 1, 3),
+]
+ON_SCALAR = [(), (0, 1), (), (0, 1), (), (0, 1), (), (0, 1), (), (1,), (), (1,), (0, 1), (), (0,), ()]
+VECTOR_EVACS = (24, 25, 28, 29)
+RAW_BUFS = {512: 4, 1024: 3, 2048: 4}
+GRP_BUFS = 3
 STAGE_BUFS = 6
 LAG = 1
-PINNED = False
 
 
 def tile_groupedlinear_kernel(tc, x, W, b, grad_out, out):
@@ -34,36 +43,25 @@ def tile_groupedlinear_kernel(tc, x, W, b, grad_out, out):
 
     with ExitStack() as ctx:
         raw_pools = {}
-        for n in (1, 2, 4):
-            raw_pools[n] = ctx.enter_context(tc.tile_pool(name="raw%d" % n, bufs=RAW_BUFS[n]))
+        for w in RAW_BUFS:
+            raw_pools[w] = ctx.enter_context(tc.tile_pool(name="raw%d" % w, bufs=RAW_BUFS[w]))
         keep = ctx.enter_context(tc.tile_pool(name="keep", bufs=1))
         grp_pool = ctx.enter_context(tc.tile_pool(name="grp", bufs=GRP_BUFS))
         stage_pool = ctx.enter_context(tc.tile_pool(name="stage", bufs=STAGE_BUFS))
         psum = ctx.enter_context(tc.psum_pool(name="psum", bufs=8))
-        if PINNED:
-            ctx.enter_context(tc.manual_schedule())
 
         codes = {}
         planes = {}
-        for kind, c, half, n in CHUNKS:
-            for j in range(2):
-                codes[(kind, c, half, j)] = keep.tile(
-                    [P, 1024], U32, name="codes_%s%d%d%d" % (kind, c, half, j), align_bytes=64)
-                planes[(kind, c, half, j)] = keep.tile(
-                    [P, 1024], U8, name="plane_%s%d%d%d" % (kind, c, half, j), align_bytes=64)
+        for n in range(len(UNITS)):
+            codes[UNITS[n]] = keep.tile([P, 1024], U32, name="codes_%d" % n, align_bytes=64)
+            planes[UNITS[n]] = keep.tile([P, 1024], U8, name="plane_%d" % n, align_bytes=64)
 
-        raws = {}
-        for k in range(len(CHUNKS)):
-            kind, c, half, n = CHUNKS[k]
+        pieces = []
+        for kind, c, lo, w in LOADS:
             src = gv if kind == "g" else xv
-            w = CW // n
-            parts = []
-            for s in range(n):
-                rw = raw_pools[n].tile([P, PACK, w], BF16, name="raw%d" % n)
-                lo = half * CW + s * w
-                nc.sync.dma_start(out=rw[:], in_=src[c][:, :, lo:lo + w])
-                parts.append(rw)
-            raws[k] = parts
+            rw = raw_pools[w].tile([P, PACK, w], BF16, name="raw%d" % w)
+            nc.sync.dma_start(out=rw[:], in_=src[c][:, :, lo:lo + w])
+            pieces.append((kind, c, lo, w, rw))
 
         def copy(on_scalar, dst, src):
             if on_scalar:
@@ -73,22 +71,29 @@ def tile_groupedlinear_kernel(tc, x, W, b, grad_out, out):
 
         grouped = {}
 
-        def regroup(k, j):
-            kind, c, half, n = CHUNKS[k]
+        def regroup(n):
+            unit = UNITS[n]
             gt = grp_pool.tile([P, 4096], BF16, name="grp", align_bytes=64)
-            grouped[(k, j)] = gt
-            for s in range(n):
-                for a in range(2):
-                    on_scalar = (2 * j + a) in SCALAR_COPIES[k]
-                    if kind == "g":
-                        nm = P // n
-                        sv = raws[k][s][:].rearrange("p t (m r a i) -> p r a m t i", r=2, a=2, i=4)
-                        dv = gt[:].rearrange("p (a i m t) -> p a m t i", a=2, i=4, t=PACK)
-                        copy(on_scalar, dv[:, a, s * nm:(s + 1) * nm], sv[:, j, a])
-                    else:
-                        sv = raws[k][s][:].rearrange("p t (g c i) -> p g c t i", g=4, i=4)
-                        dv = gt[:].rearrange("p (g c i t) -> p g c t i", g=2, i=4, t=PACK)
-                        copy(on_scalar, dv[:, a], sv[:, 2 * j + a])
+            grouped[unit] = gt
+            if unit[0] == "g":
+                c, q, r = unit[1:]
+                dv = gt[:].rearrange("p (a i m t) -> p a m t i", a=2, i=4, t=PACK)
+                for kind, pc, lo, w, rw in pieces:
+                    if kind != "g" or pc != c or lo // 2048 != q:
+                        continue
+                    m0 = (lo - 2048 * q) // 16
+                    sv = rw[:].rearrange("p t (m r a i) -> p r a m t i", r=2, a=2, i=4)
+                    for a in range(2):
+                        copy(a in ON_SCALAR[n], dv[:, a, m0:m0 + w // 16], sv[:, r, a])
+            else:
+                c, pair = unit[1:]
+                dv = gt[:].rearrange("p (g c i t) -> p g c t i", g=2, i=4, t=PACK)
+                for kind, pc, lo, w, rw in pieces:
+                    if kind != "x" or pc != c or not lo <= 1024 * pair < lo + w:
+                        continue
+                    sv = rw[:].rearrange("p t (g c i) -> p g c t i", c=P, i=4)
+                    for a in range(2):
+                        copy(a in ON_SCALAR[n], dv[:, a], sv[:, (1024 * pair - lo) // 512 + a])
 
         ready = set()
         stored = set()
@@ -99,7 +104,7 @@ def tile_groupedlinear_kernel(tc, x, W, b, grad_out, out):
                 for q in range(2):
                     if (g, q) in stored:
                         continue
-                    need = [("x", c, g // 4, (g % 4) // 2, g % 2) for c in range(2)]
+                    need = [("x", c, g // 2, g % 2) for c in range(2)]
                     need += [("g", c, q, r, a) for c in range(2) for r in range(2) for a in range(2)]
                     if not all(u in ready for u in need):
                         continue
@@ -108,7 +113,7 @@ def tile_groupedlinear_kernel(tc, x, W, b, grad_out, out):
                     for r in range(2):
                         acc = psum.tile([P, 512], F32, name="acc")
                         for c in range(2):
-                            kx = ("x", c, g // 4, (g % 4) // 2)
+                            kx = ("x", c, g // 2)
                             kg = ("g", c, q, r)
                             xs = slice((g % 2) * 512, (g % 2) * 512 + 512)
                             gs = slice(g * P, (g + 1) * P)
@@ -125,29 +130,26 @@ def tile_groupedlinear_kernel(tc, x, W, b, grad_out, out):
                         count[0] += 1
                     nc.sync.dma_start(out=ov[g, q], in_=st[:])
 
-        def quantise(k, j):
-            kind, c, half, n = CHUNKS[k]
-            fmt = E5M2 if kind == "g" else E4M3
-            key = (kind, c, half, j)
-            last = k == len(CHUNKS) - 1 and j == 1
-            pieces = 2 if last else 1
-            w = 1024 // pieces
-            for h in range(pieces):
+        def quantise(n):
+            unit = UNITS[n]
+            fmt = E5M2 if unit[0] == "g" else E4M3
+            parts = 2 if n == len(UNITS) - 1 else 1
+            w = 1024 // parts
+            for h in range(parts):
                 nc.vector.quantize_mx(
-                    out=codes[key][:, h * w:(h + 1) * w].bitcast(fmt),
-                    scales=planes[key][:, h * w:(h + 1) * w],
-                    in_=grouped[(k, j)][:, 4 * h * w:4 * (h + 1) * w],
+                    out=codes[unit][:, h * w:(h + 1) * w].bitcast(fmt),
+                    scales=planes[unit][:, h * w:(h + 1) * w],
+                    in_=grouped[unit][:, 4 * h * w:4 * (h + 1) * w],
                 )
-                if pieces == 2:
-                    ready.add(key + (h,))
+                if parts == 2:
+                    ready.add(unit + (h,))
                 else:
-                    ready.add(key + (0,))
-                    ready.add(key + (1,))
+                    ready.add(unit + (0,))
+                    ready.add(unit + (1,))
                 products()
 
-        units = [(k, j) for k in range(len(CHUNKS)) for j in range(2)]
-        for u in range(len(units) + LAG):
-            if u < len(units):
-                regroup(units[u][0], units[u][1])
-            if u >= LAG:
-                quantise(units[u - LAG][0], units[u - LAG][1])
+        for n in range(len(UNITS) + LAG):
+            if n < len(UNITS):
+                regroup(n)
+            if n >= LAG:
+                quantise(n - LAG)

@@ -16,9 +16,8 @@ P = 128
 PACK = 4
 
 LOADS = [
-    ("g", 0, 0, 512), ("g", 0, 512, 512), ("g", 0, 1024, 512), ("g", 0, 1536, 512),
-    ("g", 1, 0, 1024), ("g", 1, 1024, 1024), ("x", 0, 0, 2048), ("x", 1, 0, 2048),
-    ("g", 0, 2048, 2048), ("g", 1, 2048, 2048),
+    ("g", 0, 0, 1024), ("g", 0, 1024, 1024), ("g", 1, 0, 1024), ("g", 1, 1024, 1024),
+    ("x", 0, 0, 2048), ("x", 1, 0, 2048), ("g", 0, 2048, 2048), ("g", 1, 2048, 2048),
     ("x", 0, 2048, 1024), ("x", 1, 2048, 1024), ("x", 0, 3072, 1024), ("x", 1, 3072, 1024),
 ]
 UNITS = [
@@ -28,8 +27,8 @@ UNITS = [
     ("x", 0, 2), ("x", 1, 2), ("x", 0, 3), ("x", 1, 3),
 ]
 ON_SCALAR = [(), (0, 1), (), (0, 1), (), (0, 1), (), (0, 1), (), (1,), (), (1,), (0, 1), (), (0,), ()]
-VECTOR_EVACS = (24, 25, 28, 29)
-RAW_BUFS = {512: 4, 1024: 3, 2048: 4}
+VECTOR_EVACS = (9, 24, 25, 28, 29)
+RAW_BUFS = {1024: 5, 2048: 4}
 GRP_BUFS = 3
 STAGE_BUFS = 6
 LAG = 1

@@ -30,7 +30,7 @@ ON_SCALAR = [(), (0, 1), (), (0, 1), (), (0, 1), (), (0, 1), (), (1,), (), (1,),
 VECTOR_EVACS = (9, 24, 25, 28, 29)
 RAW_BUFS = {1024: 5, 2048: 4}
 GRP_BUFS = 3
-STAGE_BUFS = 6
+STAGE_BUFS = 12
 LAG = 1
 
 
@@ -38,7 +38,7 @@ def tile_groupedlinear_kernel(tc, x, W, b, grad_out, out):
     nc = tc.nc
     xv = x.flatten_outer_dims().rearrange("(c p t) f -> c p t f", p=P, t=PACK)
     gv = grad_out.flatten_outer_dims().rearrange("(c p t) f -> c p t f", p=P, t=PACK)
-    ov = out.rearrange("g (q m r) i -> g q m (r i)", q=2, r=2)
+    ov = out.rearrange("g (q m r) i -> g q r m i", q=2, r=2)
 
     with ExitStack() as ctx:
         raw_pools = {}
@@ -108,7 +108,6 @@ def tile_groupedlinear_kernel(tc, x, W, b, grad_out, out):
                     if not all(u in ready for u in need):
                         continue
                     stored.add((g, q))
-                    st = stage_pool.tile([P, 1024], F32, name="stage")
                     for r in range(2):
                         acc = psum.tile([P, 512], F32, name="acc")
                         for c in range(2):
@@ -125,9 +124,10 @@ def tile_groupedlinear_kernel(tc, x, W, b, grad_out, out):
                                 start=(c == 0),
                                 stop=(c == 1),
                             )
-                        copy(count[0] not in VECTOR_EVACS, st[:, r * 512:(r + 1) * 512], acc[:])
+                        st = stage_pool.tile([P, 512], F32, name="stage")
+                        copy(count[0] not in VECTOR_EVACS, st[:], acc[:])
                         count[0] += 1
-                    nc.sync.dma_start(out=ov[g, q], in_=st[:])
+                        nc.sync.dma_start(out=ov[g, q, r], in_=st[:])
 
         def quantise(n):
             unit = UNITS[n]

@@ -1,6 +1,7 @@
 from contextlib import ExitStack
 
 import concourse.mybir as mybir
+from concourse.masks import make_identity
 
 FLOPS = 2 * 8 * 512 * 512 * 1024
 BYTES = 3 * 8 * 1024 * 1024
@@ -32,6 +33,7 @@ RAW_BUFS = {1024: 5, 2048: 4}
 GRP_BUFS = 3
 STAGE_BUFS = 12
 LAG = 1
+VIA_PSUM = (5, 7)
 
 
 def tile_groupedlinear_kernel(tc, x, W, b, grad_out, out):
@@ -54,6 +56,9 @@ def tile_groupedlinear_kernel(tc, x, W, b, grad_out, out):
         for n in range(len(UNITS)):
             codes[UNITS[n]] = keep.tile([P, 1024], U32, name="codes_%d" % n, align_bytes=64)
             planes[UNITS[n]] = keep.tile([P, 1024], U8, name="plane_%d" % n, align_bytes=64)
+
+        ident = keep.tile([P, P], BF16, name="ident")
+        make_identity(nc, ident[:])
 
         pieces = []
         for kind, c, lo, w in LOADS:
@@ -89,6 +94,21 @@ def tile_groupedlinear_kernel(tc, x, W, b, grad_out, out):
                 dv = gt[:].rearrange("p (g c i t) -> p g c t i", g=2, i=4, t=PACK)
                 for kind, pc, lo, w, rw in pieces:
                     if kind != "x" or pc != c or not lo <= 1024 * pair < lo + w:
+                        continue
+                    if n in VIA_PSUM:
+                        c0 = 1024 * pair - lo
+                        for bk in range(4):
+                            ps = psum.tile([P, 1024], BF16, name="acc")
+                            pv = ps[:].rearrange("p (c u e) -> p u c e", u=2, e=2)
+                            for u in range(2):
+                                nc.tensor.matmul(
+                                    out=pv[:, u],
+                                    lhsT=ident[:],
+                                    rhs=rw[:, 2 * u:2 * u + 2, c0 + 256 * bk:c0 + 256 * (bk + 1)].rearrange("p e c -> p c e"),
+                                    start=True,
+                                    stop=True,
+                                )
+                            nc.scalar.copy(out=gt[:, 1024 * bk:1024 * (bk + 1)], in_=ps[:])
                         continue
                     sv = rw[:].rearrange("p t (g c i) -> p g c t i", c=P, i=4)
                     for a in range(2):

@@ -91,7 +91,7 @@ def tile_groupedlinear_kernel(tc, x, W, b, grad_out, out):
                         copy(a in ON_SCALAR[n], dv[:, a, m0:m0 + w // 16], sv[:, r, a])
             else:
                 c, pair = unit[1:]
-                dv = gt[:].rearrange("p (g c i t) -> p g c t i", g=2, i=4, t=PACK)
+                dv = gt[:].rearrange("p (g c i t) -> p g c t i", g=2, i=8, t=PACK)
                 for kind, pc, lo, w, rw in pieces:
                     if kind != "x" or pc != c or not lo <= 1024 * pair < lo + w:
                         continue
@@ -99,18 +99,18 @@ def tile_groupedlinear_kernel(tc, x, W, b, grad_out, out):
                         c0 = 1024 * pair - lo
                         for bk in range(4):
                             ps = psum.tile([P, 1024], BF16, name="acc")
-                            pv = ps[:].rearrange("p (c u e) -> p u c e", u=2, e=2)
+                            pv = ps[:].rearrange("p (c u e) -> p u e c", u=2, e=2)
                             for u in range(2):
                                 nc.tensor.matmul(
                                     out=pv[:, u],
                                     lhsT=ident[:],
-                                    rhs=rw[:, 2 * u:2 * u + 2, c0 + 256 * bk:c0 + 256 * (bk + 1)].rearrange("p e c -> p c e"),
+                                    rhs=rw[:, 2 * u:2 * u + 2, c0 + 256 * bk:c0 + 256 * (bk + 1)],
                                     start=True,
                                     stop=True,
                                 )
                             nc.scalar.copy(out=gt[:, 1024 * bk:1024 * (bk + 1)], in_=ps[:])
                         continue
-                    sv = rw[:].rearrange("p t (g c i) -> p g c t i", c=P, i=4)
+                    sv = rw[:].rearrange("p t (g c i) -> p g c t i", c=64, i=8)
                     for a in range(2):
                         copy(a in ON_SCALAR[n], dv[:, a], sv[:, (1024 * pair - lo) // 512 + a])
 

@@ -28,12 +28,12 @@ UNITS = [
     ("x", 0, 2), ("x", 1, 2), ("x", 0, 3), ("x", 1, 3),
 ]
 ON_SCALAR = [(), (0, 1), (), (0, 1), (), (0, 1), (), (0, 1), (), (1,), (), (1,), (0, 1), (), (0,), ()]
-VECTOR_EVACS = (9, 24, 25, 28, 29)
+VECTOR_EVACS = (24, 25, 28, 29)
 RAW_BUFS = {1024: 5, 2048: 4}
 GRP_BUFS = 3
 STAGE_BUFS = 12
 LAG = 1
-VIA_PSUM = (5, 7)
+VIA_PSUM = (5, 7, 12)
 
 
 def tile_groupedlinear_kernel(tc, x, W, b, grad_out, out):

@@ -27,7 +27,7 @@ UNITS = [
     ("g", 0, 1, 0), ("g", 0, 1, 1), ("g", 1, 1, 0), ("g", 1, 1, 1),
     ("x", 0, 2), ("x", 1, 2), ("x", 0, 3), ("x", 1, 3),
 ]
-ON_SCALAR = [(), (0, 1), (), (0, 1), (), (0, 1), (), (0, 1), (), (1,), (), (1,), (0, 1), (), (0,), ()]
+ON_SCALAR = [(), (0, 1), (), (0, 1), (), (0, 1), (1,), (0, 1), (), (1,), (), (1,), (0, 1), (), (0,), ()]
 VECTOR_EVACS = (24, 25, 28, 29)
 RAW_BUFS = {1024: 5, 2048: 4}
 GRP_BUFS = 3

@@ -108,7 +108,7 @@ def tile_groupedlinear_kernel(tc, x, W, b, grad_out, out):
                                     start=True,
                                     stop=True,
                                 )
-                            nc.scalar.copy(out=gt[:, 1024 * bk:1024 * (bk + 1)], in_=ps[:])
+                            nc.scalar.copy(out=gt[:, 1024 * bk:1024 * (bk + 1)].bitcast(F32), in_=ps[:].bitcast(F32))
                         continue
                     sv = rw[:].rearrange("p t (g c i) -> p g c t i", c=64, i=8)
                     for a in range(2):

@@ -31,7 +31,7 @@ ON_SCALAR = [(), (0, 1), (), (0, 1), (), (0, 1), (1,), (0, 1), (), (1,), (), (1,
 VECTOR_EVACS = (24, 25, 28, 29)
 RAW_BUFS = {1024: 5, 2048: 4}
 GRP_BUFS = 3
-STAGE_BUFS = 12
+STAGE_BUFS = 7
 LAG = 1
 VIA_PSUM = (5, 7, 12)
 
@@ -41,6 +41,7 @@ def tile_groupedlinear_kernel(tc, x, W, b, grad_out, out):
     xv = x.flatten_outer_dims().rearrange("(c p t) f -> c p t f", p=P, t=PACK)
     gv = grad_out.flatten_outer_dims().rearrange("(c p t) f -> c p t f", p=P, t=PACK)
     ov = out.rearrange("g (q m r) i -> g q r m i", q=2, r=2)
+    ow = out.rearrange("g (q m r) i -> g q m (r i)", q=2, r=2)
 
     with ExitStack() as ctx:
         raw_pools = {}
@@ -128,6 +129,7 @@ def tile_groupedlinear_kernel(tc, x, W, b, grad_out, out):
                     if not all(u in ready for u in need):
                         continue
                     stored.add((g, q))
+                    st = stage_pool.tile([P, 1024], F32, name="stage")
                     for r in range(2):
                         acc = psum.tile([P, 512], F32, name="acc")
                         for c in range(2):
@@ -144,10 +146,12 @@ def tile_groupedlinear_kernel(tc, x, W, b, grad_out, out):
                                 start=(c == 0),
                                 stop=(c == 1),
                             )
-                        st = stage_pool.tile([P, 512], F32, name="stage")
-                        copy(count[0] not in VECTOR_EVACS, st[:], acc[:])
+                        copy(count[0] not in VECTOR_EVACS, st[:, r * 512:(r + 1) * 512], acc[:])
                         count[0] += 1
-                        nc.sync.dma_start(out=ov[g, q, r], in_=st[:])
+                        if g >= 6:
+                            nc.sync.dma_start(out=ov[g, q, r], in_=st[:, r * 512:(r + 1) * 512])
+                    if g < 6:
+                        nc.sync.dma_start(out=ow[g, q], in_=st[:])
 
         def quantise(n):
             unit = UNITS[n]

from contextlib import ExitStack

import concourse.mybir as mybir
from concourse.masks import make_identity

FLOPS = 2 * 8 * 512 * 512 * 1024
BYTES = 3 * 8 * 1024 * 1024

BF16 = mybir.dt.bfloat16
F32 = mybir.dt.float32
U32 = mybir.dt.uint32
U8 = mybir.dt.uint8
E4M3 = mybir.dt.float8_e4m3fn_x4
E5M2 = mybir.dt.float8_e5m2_x4

P = 128
PACK = 4

LOADS = [
    ("g", 0, 0, 1024), ("g", 0, 1024, 1024), ("g", 1, 0, 1024), ("g", 1, 1024, 1024),
    ("x", 0, 0, 2048), ("x", 1, 0, 2048), ("g", 0, 2048, 2048), ("g", 1, 2048, 2048),
    ("x", 0, 2048, 1024), ("x", 1, 2048, 1024), ("x", 0, 3072, 1024), ("x", 1, 3072, 1024),
]
UNITS = [
    ("g", 0, 0, 0), ("g", 0, 0, 1), ("g", 1, 0, 0), ("g", 1, 0, 1),
    ("x", 0, 0), ("x", 0, 1), ("x", 1, 0), ("x", 1, 1),
    ("g", 0, 1, 0), ("g", 0, 1, 1), ("g", 1, 1, 0), ("g", 1, 1, 1),
    ("x", 0, 2), ("x", 1, 2), ("x", 0, 3), ("x", 1, 3),
]
ON_SCALAR = [(), (0, 1), (), (0, 1), (), (0, 1), (1,), (0, 1), (), (1,), (), (1,), (0, 1), (), (0,), ()]
VECTOR_EVACS = (24, 25, 28, 29)
RAW_BUFS = {1024: 5, 2048: 4}
GRP_BUFS = 3
STAGE_BUFS = 7
LAG = 1
VIA_PSUM = (5, 7, 12)


def tile_groupedlinear_kernel(tc, x, W, b, grad_out, out):
    nc = tc.nc
    xv = x.flatten_outer_dims().rearrange("(c p t) f -> c p t f", p=P, t=PACK)
    gv = grad_out.flatten_outer_dims().rearrange("(c p t) f -> c p t f", p=P, t=PACK)
    ov = out.rearrange("g (q m r) i -> g q r m i", q=2, r=2)
    ow = out.rearrange("g (q m r) i -> g q m (r i)", q=2, r=2)

    with ExitStack() as ctx:
        raw_pools = {}
        for w in RAW_BUFS:
            raw_pools[w] = ctx.enter_context(tc.tile_pool(name="raw%d" % w, bufs=RAW_BUFS[w]))
        keep = ctx.enter_context(tc.tile_pool(name="keep", bufs=1))
        grp_pool = ctx.enter_context(tc.tile_pool(name="grp", bufs=GRP_BUFS))
        stage_pool = ctx.enter_context(tc.tile_pool(name="stage", bufs=STAGE_BUFS))
        psum = ctx.enter_context(tc.psum_pool(name="psum", bufs=8))

        codes = {}
        planes = {}
        for n in range(len(UNITS)):
            codes[UNITS[n]] = keep.tile([P, 1024], U32, name="codes_%d" % n, align_bytes=64)
            planes[UNITS[n]] = keep.tile([P, 1024], U8, name="plane_%d" % n, align_bytes=64)

        ident = keep.tile([P, P], BF16, name="ident")
        make_identity(nc, ident[:])

        pieces = []
        for kind, c, lo, w in LOADS:
            src = gv if kind == "g" else xv
            rw = raw_pools[w].tile([P, PACK, w], BF16, name="raw%d" % w)
            nc.sync.dma_start(out=rw[:], in_=src[c][:, :, lo:lo + w])
            pieces.append((kind, c, lo, w, rw))

        def copy(on_scalar, dst, src):
            if on_scalar:
                nc.scalar.copy(out=dst, in_=src)
            else:
                nc.vector.tensor_copy(out=dst, in_=src)

        grouped = {}

        def regroup(n):
            unit = UNITS[n]
            gt = grp_pool.tile([P, 4096], BF16, name="grp", align_bytes=64)
            grouped[unit] = gt
            if unit[0] == "g":
                c, q, r = unit[1:]
                dv = gt[:].rearrange("p (a i m t) -> p a m t i", a=2, i=4, t=PACK)
                for kind, pc, lo, w, rw in pieces:
                    if kind != "g" or pc != c or lo // 2048 != q:
                        continue
                    m0 = (lo - 2048 * q) // 16
                    sv = rw[:].rearrange("p t (m r a i) -> p r a m t i", r=2, a=2, i=4)
                    for a in range(2):
                        copy(a in ON_SCALAR[n], dv[:, a, m0:m0 + w // 16], sv[:, r, a])
            else:
                c, pair = unit[1:]
                dv = gt[:].rearrange("p (g c i t) -> p g c t i", g=2, i=8, t=PACK)
                for kind, pc, lo, w, rw in pieces:
                    if kind != "x" or pc != c or not lo <= 1024 * pair < lo + w:
                        continue
                    if n in VIA_PSUM:
                        c0 = 1024 * pair - lo
                        for bk in range(4):
                            ps = psum.tile([P, 1024], BF16, name="acc")
                            pv = ps[:].rearrange("p (c u e) -> p u e c", u=2, e=2)
                            for u in range(2):
                                nc.tensor.matmul(
                                    out=pv[:, u],
                                    lhsT=ident[:],
                                    rhs=rw[:, 2 * u:2 * u + 2, c0 + 256 * bk:c0 + 256 * (bk + 1)],
                                    start=True,
                                    stop=True,
                                )
                            nc.scalar.copy(out=gt[:, 1024 * bk:1024 * (bk + 1)].bitcast(F32), in_=ps[:].bitcast(F32))
                        continue
                    sv = rw[:].rearrange("p t (g c i) -> p g c t i", c=64, i=8)
                    for a in range(2):
                        copy(a in ON_SCALAR[n], dv[:, a], sv[:, (1024 * pair - lo) // 512 + a])

        ready = set()
        stored = set()
        count = [0]

        def products():
            for g in range(8):
                for q in range(2):
                    if (g, q) in stored:
                        continue
                    need = [("x", c, g // 2, g % 2) for c in range(2)]
                    need += [("g", c, q, r, a) for c in range(2) for r in range(2) for a in range(2)]
                    if not all(u in ready for u in need):
                        continue
                    stored.add((g, q))
                    st = stage_pool.tile([P, 1024], F32, name="stage")
                    for r in range(2):
                        acc = psum.tile([P, 512], F32, name="acc")
                        for c in range(2):
                            kx = ("x", c, g // 2)
                            kg = ("g", c, q, r)
                            xs = slice((g % 2) * 512, (g % 2) * 512 + 512)
                            gs = slice(g * P, (g + 1) * P)
                            nc.tensor.matmul_mx(
                                out=acc[:],
                                lhsT=codes[kg][:, gs].bitcast(E5M2),
                                lhsT_scale=planes[kg][:, gs],
                                rhs=codes[kx][:, xs].bitcast(E4M3),
                                rhs_scale=planes[kx][:, xs],
                                start=(c == 0),
                                stop=(c == 1),
                            )
                        copy(count[0] not in VECTOR_EVACS, st[:, r * 512:(r + 1) * 512], acc[:])
                        count[0] += 1
                        if g >= 6:
                            nc.sync.dma_start(out=ov[g, q, r], in_=st[:, r * 512:(r + 1) * 512])
                    if g < 6:
                        nc.sync.dma_start(out=ow[g, q], in_=st[:])

        def quantise(n):
            unit = UNITS[n]
            fmt = E5M2 if unit[0] == "g" else E4M3
            parts = 2 if n == len(UNITS) - 1 else 1
            w = 1024 // parts
            for h in range(parts):
                nc.vector.quantize_mx(
                    out=codes[unit][:, h * w:(h + 1) * w].bitcast(fmt),
                    scales=planes[unit][:, h * w:(h + 1) * w],
                    in_=grouped[unit][:, 4 * h * w:4 * (h + 1) * w],
                )
                if parts == 2:
                    ready.add(unit + (h,))
                else:
                    ready.add(unit + (0,))
                    ready.add(unit + (1,))
                products()

        for n in range(len(UNITS) + LAG):
            if n < len(UNITS):
                regroup(n)
            if n >= LAG:
                quantise(n - LAG)
